import numpy as np
import ml_dtypes

BF16 = ml_dtypes.bfloat16


def bf(x):
    return np.asarray(x, np.float32).astype(BF16)


def f32(x):
    return np.asarray(x, np.float32)


def f64(x):
    return np.asarray(x).astype(np.float64)


def striped(idx):
    return np.tile(idx.reshape(-1, 16).T, (8, 1))


D, S, N, NK, F, M = 128, 2048, 1024, 2, 896, 512
TAU = 0.5


def setup_inputs():
    return {
        "x": bf(np.random.standard_normal((D, S))),
        "lt": bf(np.random.standard_normal((S, S)) / np.sqrt(S)),
        "kt": bf(np.random.standard_normal((NK, N, N)) / np.sqrt(N)),
        "w": bf(np.random.standard_normal((F, M)) / np.sqrt(F)),
        "b": f32(0.1 * np.random.standard_normal((M, 1))),
        "offs": striped(np.random.permutation(S)[:N]),
    }


def reference(x, lt, kt, w, b, offs):
    idx = offs[:16].T.reshape(-1)
    x, lt, kt, w, b = f64(x), f64(lt), f64(kt), f64(w), f64(b)
    xd = x - TAU * (x @ lt)
    h0 = xd[:, idx]
    h1 = np.concatenate([h0 @ kt[a] for a in range(NK)], axis=0)
    h2 = np.concatenate([h1 @ kt[a] for a in range(NK)], axis=0)
    cat = np.concatenate([h0, h1, h2], axis=0)
    return np.tanh(w.T @ cat + b)

@@ -1,0 +1,183 @@
+from contextlib import ExitStack
+
+import concourse.mybir as mybir
+from concourse.masks import make_identity
+
+P = 128
+S = 2048
+N = 1024
+NK = 2
+M = 512
+TAU = 0.5
+COLS = 512
+QUAD = COLS // P
+
+S_BLOCKS = S // P
+S_PIECES = S // COLS
+N_BLOCKS = N // P
+N_PIECES = N // COLS
+M_BLOCKS = M // P
+CAT_BLOCKS = 1 + NK + NK * NK
+LT_ROWS = 2
+
+FLOPS = 2 * (P * S * S + NK * P * N * N + NK * NK * P * N * N + CAT_BLOCKS * P * M * N)
+
+BF16, F32, U16 = mybir.dt.bfloat16, mybir.dt.float32, mybir.dt.uint16
+MULT, ADD = mybir.AluOpType.mult, mybir.AluOpType.add
+TANH = mybir.ActivationFunctionType.Tanh
+
+
+def piece(n):
+    return slice(n * COLS, (n + 1) * COLS)
+
+
+def block(n):
+    return slice(n * P, (n + 1) * P)
+
+
+def tile_net_b_kernel(tc, x, lt, kt, w, b, offs, out):
+    nc = tc.nc
+    with ExitStack() as ctx:
+        held = ctx.enter_context(tc.tile_pool(name="held", bufs=1))
+        staged = ctx.enter_context(tc.tile_pool(name="staged", bufs=4))
+        long_banks = ctx.enter_context(tc.psum_pool(name="long_banks", bufs=4))
+        hop_banks = ctx.enter_context(tc.psum_pool(name="hop_banks", bufs=2))
+        flip_banks = ctx.enter_context(tc.psum_pool(name="flip_banks", bufs=2))
+
+        offsets = held.tile([P, N // 16], U16, name="offsets")
+        nc.sync.dma_start(offsets[:], offs)
+        x_sb = held.tile([P, S], BF16, name="x_sb")
+        nc.scalar.dma_start(x_sb[:], x)
+
+        lt_loads = lt.rearrange("(c k p) s -> c p k s", k=LT_ROWS, p=P)
+        lt_sb = []
+        for c in range(S_BLOCKS // LT_ROWS):
+            lt_tile = held.tile([P, LT_ROWS, S], BF16, name=f"lt{c}")
+            queue = nc.sync if c % 2 == 0 else nc.scalar
+            queue.dma_start(lt_tile[:], lt_loads[c])
+            lt_sb.append(lt_tile)
+
+        w_h0 = held.tile([P, M], BF16, name="w_h0")
+        nc.sync.dma_start(w_h0[:], w[0:P, :])
+
+        kt_sb = []
+        for a in range(NK):
+            kt_loads = kt[a].rearrange("(h k p) j -> h p k j", k=QUAD, p=P)
+            halves = []
+            for h in range(N_BLOCKS // QUAD):
+                kt_tile = held.tile([P, QUAD, N], BF16, name=f"kt{a}{h}")
+                queue = nc.sync if h % 2 == 0 else nc.scalar
+                queue.dma_start(kt_tile[:], kt_loads[h])
+                halves.append(kt_tile)
+            kt_sb.append(halves)
+
+        w_rest = held.tile([P, CAT_BLOCKS - 1, M], BF16, name="w_rest")
+        nc.sync.dma_start(w_rest[:], w[P : CAT_BLOCKS * P, :].rearrange("(f p) m -> p f m", p=P))
+        bias = held.tile([P, M_BLOCKS], F32, name="bias")
+        with nc.allow_non_contiguous_dma(reason="one bias value to a partition"):
+            nc.gpsimd.dma_start(bias[:], b.rearrange("(a p) o -> p (a o)", p=P))
+
+        identity = held.tile([P, P], BF16, name="identity")
+        make_identity(nc, identity[:])
+
+        def flipped(source, name):
+            bank = flip_banks.tile([P, QUAD, P], BF16, name="flip_bank")
+            for q in range(QUAD):
+                nc.tensor.transpose(bank[:, q, :], source[:, block(q)], identity[:])
+            result = held.tile([P, QUAD, P], BF16, name=name)
+            nc.scalar.copy(result[:], bank[:])
+            return result
+
+        xT = [flipped(x_sb[:, piece(g)], f"xT{g}") for g in range(S_PIECES)]
+
+        xd_banks = [long_banks.tile([P, COLS], F32, name=f"xd_bank{s}", tag="long") for s in range(S_PIECES)]
+        for c in range(S_BLOCKS // LT_ROWS):
+            for s in range(S_PIECES):
+                for k in range(LT_ROWS):
+                    t = c * LT_ROWS + k
+                    nc.tensor.matmul(
+                        xd_banks[s][:],
+                        xT[t // QUAD][:, t % QUAD, :],
+                        lt_sb[c][:, k, piece(s)],
+                        start=(t == 0),
+                        stop=(t == S_BLOCKS - 1),
+                    )
+        xd = held.tile([P, S], BF16, name="xd")
+        for s in range(S_PIECES):
+            nc.vector.scalar_tensor_tensor(
+                out=xd[:, piece(s)], in0=xd_banks[s][:], scalar=-TAU, in1=x_sb[:, piece(s)], op0=MULT, op1=ADD
+            )
+
+        def picked(j):
+            return xd[:].indirect(offsets[:, j * (COLS // 16) : (j + 1) * (COLS // 16)])
+
+        def open_encoder(j):
+            banks = []
+            for m in range(M_BLOCKS):
+                bank = long_banks.tile([P, COLS], F32, name=f"out_bank{m}", tag="long")
+                nc.tensor.matmul(bank[:], w_h0[:, block(m)], picked(j), start=True, stop=False)
+                banks.append(bank)
+            return banks
+
+        def close_encoder(j, banks, layers):
+            for m in range(M_BLOCKS):
+                for f, layer in enumerate(layers):
+                    nc.tensor.matmul(
+                        banks[m][:], w_rest[:, f, block(m)], layer[j][:], start=False, stop=(f == len(layers) - 1)
+                    )
+                out_sb = staged.tile([P, COLS], F32, name="out_sb")
+                nc.scalar.activation(out_sb[:], banks[m][:], TANH, bias=bias[:, m : m + 1])
+                nc.sync.dma_start(out[block(m), piece(j)], out_sb[:])
+
+        def hop(flipped_pieces, a, j, name):
+            bank = hop_banks.tile([P, COLS], F32, name="hop_bank")
+            for i in range(N_BLOCKS):
+                nc.tensor.matmul(
+                    bank[:],
+                    flipped_pieces[i // QUAD][:, i % QUAD, :],
+                    kt_sb[a][i // QUAD][:, i % QUAD, piece(j)],
+                    start=(i == 0),
+                    stop=(i == N_BLOCKS - 1),
+                )
+            result = held.tile([P, COLS], BF16, name=name)
+            nc.vector.tensor_copy(result[:], bank[:])
+            return result
+
+        h0_banks = []
+        for j in range(N_PIECES):
+            bank = hop_banks.tile([P, COLS], F32, name="hop_bank")
+            nc.tensor.matmul(bank[:], identity[:], picked(j), start=True, stop=True)
+            h0_banks.append(bank)
+        out_banks = open_encoder(0)
+        h0T = []
+        for j in range(N_PIECES):
+            h0 = held.tile([P, COLS], BF16, name=f"h0_{j}")
+            nc.vector.tensor_copy(h0[:], h0_banks[j][:])
+            h0T.append(flipped(h0, f"h0T{j}"))
+
+        h1 = [[None] * N_PIECES for a in range(NK)]
+        h1T = [[None] * N_PIECES for a in range(NK)]
+        late = []
+
+        def flip_oldest():
+            a, j = late[0]
+            late.remove(late[0])
+            h1T[a][j] = flipped(h1[a][j], f"h1T{a}{j}")
+
+        for a in range(NK):
+            for j in range(N_PIECES):
+                h1[a][j] = hop(h0T, a, j, f"h1_{a}{j}")
+                late.append((a, j))
+                if len(late) == 2:
+                    flip_oldest()
+
+        h2 = [[None] * N_PIECES for r in range(NK * NK)]
+        for j in range(N_PIECES):
+            for e in range(NK):
+                for a in range(NK):
+                    h2[NK * a + e][j] = hop(h1T[e], a, j, f"h2_{a}{e}{j}")
+                    if late:
+                        flip_oldest()
+            if j > 0:
+                out_banks = open_encoder(j)
+            close_encoder(j, out_banks, h1 + h2)

@@ -18,12 +18,10 @@ N_BLOCKS = N // P
 N_PIECES = N // COLS
 M_BLOCKS = M // P
 CAT_BLOCKS = 1 + NK + NK * NK
-LT_ROWS = 2
 
 FLOPS = 2 * (P * S * S + NK * P * N * N + NK * NK * P * N * N + CAT_BLOCKS * P * M * N)
 
 BF16, F32, U16 = mybir.dt.bfloat16, mybir.dt.float32, mybir.dt.uint16
-MULT, ADD = mybir.AluOpType.mult, mybir.AluOpType.add
 TANH = mybir.ActivationFunctionType.Tanh
 
 
@@ -44,17 +42,21 @@ def tile_net_b_kernel(tc, x, lt, kt, w, b, offs, out):
         hop_banks = ctx.enter_context(tc.psum_pool(name="hop_banks", bufs=2))
         flip_banks = ctx.enter_context(tc.psum_pool(name="flip_banks", bufs=2))
 
+        x_sb = []
+        for s in range(S_PIECES):
+            x_piece = held.tile([P, COLS], BF16, name=f"x{s}")
+            nc.scalar.dma_start(x_piece[:], x[:, piece(s)])
+            x_sb.append(x_piece)
+        bias = held.tile([P, M_BLOCKS], F32, name="bias")
+        with nc.allow_non_contiguous_dma(reason="one bias value to a partition"):
+            nc.scalar.dma_start(bias[:], b.rearrange("(a p) o -> p (a o)", p=P))
         offsets = held.tile([P, N // 16], U16, name="offsets")
         nc.sync.dma_start(offsets[:], offs)
-        x_sb = held.tile([P, S], BF16, name="x_sb")
-        nc.scalar.dma_start(x_sb[:], x)
 
-        lt_loads = lt.rearrange("(c k p) s -> c p k s", k=LT_ROWS, p=P)
         lt_sb = []
-        for c in range(S_BLOCKS // LT_ROWS):
-            lt_tile = held.tile([P, LT_ROWS, S], BF16, name=f"lt{c}")
-            queue = nc.sync if c % 2 == 0 else nc.scalar
-            queue.dma_start(lt_tile[:], lt_loads[c])
+        for t in range(S_BLOCKS):
+            lt_tile = held.tile([P, S], BF16, name=f"lt{t}")
+            nc.sync.dma_start(lt_tile[:], lt[block(t), :])
             lt_sb.append(lt_tile)
 
         w_h0 = held.tile([P, M], BF16, name="w_h0")
@@ -66,58 +68,62 @@ def tile_net_b_kernel(tc, x, lt, kt, w, b, offs, out):
             halves = []
             for h in range(N_BLOCKS // QUAD):
                 kt_tile = held.tile([P, QUAD, N], BF16, name=f"kt{a}{h}")
-                queue = nc.sync if h % 2 == 0 else nc.scalar
-                queue.dma_start(kt_tile[:], kt_loads[h])
+                nc.sync.dma_start(kt_tile[:], kt_loads[h])
                 halves.append(kt_tile)
             kt_sb.append(halves)
 
         w_rest = held.tile([P, CAT_BLOCKS - 1, M], BF16, name="w_rest")
         nc.sync.dma_start(w_rest[:], w[P : CAT_BLOCKS * P, :].rearrange("(f p) m -> p f m", p=P))
-        bias = held.tile([P, M_BLOCKS], F32, name="bias")
-        with nc.allow_non_contiguous_dma(reason="one bias value to a partition"):
-            nc.gpsimd.dma_start(bias[:], b.rearrange("(a p) o -> p (a o)", p=P))
 
         identity = held.tile([P, P], BF16, name="identity")
         make_identity(nc, identity[:])
 
-        def flipped(source, name):
+        def copy_out(n, target, bank):
+            if n % 2 == 0:
+                nc.vector.tensor_copy(target, bank)
+            else:
+                nc.scalar.copy(target, bank)
+
+        def flip_blocks(source):
             bank = flip_banks.tile([P, QUAD, P], BF16, name="flip_bank")
             for q in range(QUAD):
                 nc.tensor.transpose(bank[:, q, :], source[:, block(q)], identity[:])
+            return bank
+
+        def flipped(n, source, name):
             result = held.tile([P, QUAD, P], BF16, name=name)
-            nc.scalar.copy(result[:], bank[:])
+            copy_out(n, result[:], flip_blocks(source)[:])
             return result
 
-        xT = [flipped(x_sb[:, piece(g)], f"xT{g}") for g in range(S_PIECES)]
-
-        xd_banks = [long_banks.tile([P, COLS], F32, name=f"xd_bank{s}", tag="long") for s in range(S_PIECES)]
-        for c in range(S_BLOCKS // LT_ROWS):
+        xd_banks = []
+        xT = []
+        for s in range(S_PIECES):
+            xd_bank = long_banks.tile([P, COLS], F32, name=f"xd_bank{s}", tag="long")
+            nc.tensor.matmul(xd_bank[:], identity[:], x_sb[s][:], start=True, stop=False)
+            xd_banks.append(xd_bank)
+            scaled = held.tile([P, QUAD, P], BF16, name=f"xT{s}")
+            nc.vector.tensor_scalar_mul(scaled[:], flip_blocks(x_sb[s])[:], -TAU)
+            xT.append(scaled)
+        for t in range(S_BLOCKS):
             for s in range(S_PIECES):
-                for k in range(LT_ROWS):
-                    t = c * LT_ROWS + k
-                    nc.tensor.matmul(
-                        xd_banks[s][:],
-                        xT[t // QUAD][:, t % QUAD, :],
-                        lt_sb[c][:, k, piece(s)],
-                        start=(t == 0),
-                        stop=(t == S_BLOCKS - 1),
-                    )
+                nc.tensor.matmul(
+                    xd_banks[s][:],
+                    xT[t // QUAD][:, t % QUAD, :],
+                    lt_sb[t][:, piece(s)],
+                    start=False,
+                    stop=(t == S_BLOCKS - 1),
+                )
         xd = held.tile([P, S], BF16, name="xd")
         for s in range(S_PIECES):
-            nc.vector.scalar_tensor_tensor(
-                out=xd[:, piece(s)], in0=xd_banks[s][:], scalar=-TAU, in1=x_sb[:, piece(s)], op0=MULT, op1=ADD
-            )
+            copy_out(s, xd[:, piece(s)], xd_banks[s][:])
 
         def picked(j):
             return xd[:].indirect(offsets[:, j * (COLS // 16) : (j + 1) * (COLS // 16)])
 
-        def open_encoder(j):
-            banks = []
-            for m in range(M_BLOCKS):
-                bank = long_banks.tile([P, COLS], F32, name=f"out_bank{m}", tag="long")
-                nc.tensor.matmul(bank[:], w_h0[:, block(m)], picked(j), start=True, stop=False)
-                banks.append(bank)
-            return banks
+        def open_encoder(j, m):
+            bank = long_banks.tile([P, COLS], F32, name=f"out_bank{m}", tag="long")
+            nc.tensor.matmul(bank[:], w_h0[:, block(m)], picked(j), start=True, stop=False)
+            return bank
 
         def close_encoder(j, banks, layers):
             for m in range(M_BLOCKS):
@@ -140,7 +146,7 @@ def tile_net_b_kernel(tc, x, lt, kt, w, b, offs, out):
                     stop=(i == N_BLOCKS - 1),
                 )
             result = held.tile([P, COLS], BF16, name=name)
-            nc.vector.tensor_copy(result[:], bank[:])
+            copy_out(j, result[:], bank[:])
             return result
 
         h0_banks = []
@@ -148,12 +154,13 @@ def tile_net_b_kernel(tc, x, lt, kt, w, b, offs, out):
             bank = hop_banks.tile([P, COLS], F32, name="hop_bank")
             nc.tensor.matmul(bank[:], identity[:], picked(j), start=True, stop=True)
             h0_banks.append(bank)
-        out_banks = open_encoder(0)
+        out_banks = [open_encoder(0, m) for m in range(M_BLOCKS // 2)]
         h0T = []
         for j in range(N_PIECES):
             h0 = held.tile([P, COLS], BF16, name=f"h0_{j}")
-            nc.vector.tensor_copy(h0[:], h0_banks[j][:])
-            h0T.append(flipped(h0, f"h0T{j}"))
+            copy_out(j, h0[:], h0_banks[j][:])
+            h0T.append(flipped(j, h0, f"h0T{j}"))
+        out_banks.extend([open_encoder(0, m) for m in range(M_BLOCKS // 2, M_BLOCKS)])
 
         h1 = [[None] * N_PIECES for a in range(NK)]
         h1T = [[None] * N_PIECES for a in range(NK)]
@@ -162,7 +169,7 @@ def tile_net_b_kernel(tc, x, lt, kt, w, b, offs, out):
         def flip_oldest():
             a, j = late[0]
             late.remove(late[0])
-            h1T[a][j] = flipped(h1[a][j], f"h1T{a}{j}")
+            h1T[a][j] = flipped(j, h1[a][j], f"h1T{a}{j}")
 
         for a in range(NK):
             for j in range(N_PIECES):
@@ -179,5 +186,5 @@ def tile_net_b_kernel(tc, x, lt, kt, w, b, offs, out):
                     if late:
                         flip_oldest()
             if j > 0:
-                out_banks = open_encoder(j)
+                out_banks = [open_encoder(j, m) for m in range(M_BLOCKS)]
             close_encoder(j, out_banks, h1 + h2)

@@ -18,6 +18,7 @@ N_BLOCKS = N // P
 N_PIECES = N // COLS
 M_BLOCKS = M // P
 CAT_BLOCKS = 1 + NK + NK * NK
+LT_PAIR = 2
 
 FLOPS = 2 * (P * S * S + NK * P * N * N + NK * NK * P * N * N + CAT_BLOCKS * P * M * N)
 
@@ -42,22 +43,22 @@ def tile_net_b_kernel(tc, x, lt, kt, w, b, offs, out):
         hop_banks = ctx.enter_context(tc.psum_pool(name="hop_banks", bufs=2))
         flip_banks = ctx.enter_context(tc.psum_pool(name="flip_banks", bufs=2))
 
-        x_sb = []
-        for s in range(S_PIECES):
-            x_piece = held.tile([P, COLS], BF16, name=f"x{s}")
-            nc.scalar.dma_start(x_piece[:], x[:, piece(s)])
-            x_sb.append(x_piece)
+        x_sb = held.tile([P, S], BF16, name="x_sb")
+        nc.scalar.dma_start(x_sb[:], x)
         bias = held.tile([P, M_BLOCKS], F32, name="bias")
         with nc.allow_non_contiguous_dma(reason="one bias value to a partition"):
             nc.scalar.dma_start(bias[:], b.rearrange("(a p) o -> p (a o)", p=P))
         offsets = held.tile([P, N // 16], U16, name="offsets")
         nc.sync.dma_start(offsets[:], offs)
 
+        lt_blocks = lt.rearrange("(p k) s -> p k s", k=S_BLOCKS)
+        first_blocks = list(range(0, S_BLOCKS - LT_PAIR, LT_PAIR)) + list(range(S_BLOCKS - LT_PAIR, S_BLOCKS))
         lt_sb = []
-        for t in range(S_BLOCKS):
-            lt_tile = held.tile([P, S], BF16, name=f"lt{t}")
-            nc.sync.dma_start(lt_tile[:], lt[block(t), :])
-            lt_sb.append(lt_tile)
+        for n, k in enumerate(first_blocks):
+            count = (first_blocks + [S_BLOCKS])[n + 1] - k
+            lt_tile = held.tile([P, count, S], BF16, name=f"lt{k}")
+            nc.sync.dma_start(lt_tile[:], lt_blocks[:, k : k + count, :])
+            lt_sb.extend([lt_tile[:, i, :] for i in range(count)])
 
         w_h0 = held.tile([P, M], BF16, name="w_h0")
         nc.sync.dma_start(w_h0[:], w[0:P, :])
@@ -84,34 +85,37 @@ def tile_net_b_kernel(tc, x, lt, kt, w, b, offs, out):
             else:
                 nc.scalar.copy(target, bank)
 
-        def flip_blocks(source):
+        def flip_blocks(blocks):
             bank = flip_banks.tile([P, QUAD, P], BF16, name="flip_bank")
             for q in range(QUAD):
-                nc.tensor.transpose(bank[:, q, :], source[:, block(q)], identity[:])
+                nc.tensor.transpose(bank[:, q, :], blocks[q], identity[:])
             return bank
 
         def flipped(n, source, name):
             result = held.tile([P, QUAD, P], BF16, name=name)
-            copy_out(n, result[:], flip_blocks(source)[:])
+            copy_out(n, result[:], flip_blocks([source[:, block(q)] for q in range(QUAD)])[:])
             return result
 
+        x_blocks = x_sb[:].rearrange("d (p k) -> d k p", k=S_BLOCKS)
         xd_banks = []
         xT = []
-        for s in range(S_PIECES):
-            xd_bank = long_banks.tile([P, COLS], F32, name=f"xd_bank{s}", tag="long")
-            nc.tensor.matmul(xd_bank[:], identity[:], x_sb[s][:], start=True, stop=False)
+        for g in range(S_PIECES):
+            xd_bank = long_banks.tile([P, COLS], F32, name=f"xd_bank{g}", tag="long")
+            nc.tensor.matmul(xd_bank[:], identity[:], x_sb[:, piece(g)], start=True, stop=False)
             xd_banks.append(xd_bank)
-            scaled = held.tile([P, QUAD, P], BF16, name=f"xT{s}")
-            nc.vector.tensor_scalar_mul(scaled[:], flip_blocks(x_sb[s])[:], -TAU)
+            scaled = held.tile([P, QUAD, P], BF16, name=f"xT{g}")
+            nc.vector.tensor_scalar_mul(
+                scaled[:], flip_blocks([x_blocks[:, QUAD * g + q, :] for q in range(QUAD)])[:], -TAU
+            )
             xT.append(scaled)
-        for t in range(S_BLOCKS):
+        for k in range(S_BLOCKS):
             for s in range(S_PIECES):
                 nc.tensor.matmul(
                     xd_banks[s][:],
-                    xT[t // QUAD][:, t % QUAD, :],
-                    lt_sb[t][:, piece(s)],
+                    xT[k // QUAD][:, k % QUAD, :],
+                    lt_sb[k][:, piece(s)],
                     start=False,
-                    stop=(t == S_BLOCKS - 1),
+                    stop=(k == S_BLOCKS - 1),
                 )
         xd = held.tile([P, S], BF16, name="xd")
         for s in range(S_PIECES):

@@ -18,11 +18,12 @@ N_BLOCKS = N // P
 N_PIECES = N // COLS
 M_BLOCKS = M // P
 CAT_BLOCKS = 1 + NK + NK * NK
-LT_PAIR = 2
+LAST = 2
 
 FLOPS = 2 * (P * S * S + NK * P * N * N + NK * NK * P * N * N + CAT_BLOCKS * P * M * N)
 
 BF16, F32, U16 = mybir.dt.bfloat16, mybir.dt.float32, mybir.dt.uint16
+MULT, ADD = mybir.AluOpType.mult, mybir.AluOpType.add
 TANH = mybir.ActivationFunctionType.Tanh
 
 
@@ -43,22 +44,22 @@ def tile_net_b_kernel(tc, x, lt, kt, w, b, offs, out):
         hop_banks = ctx.enter_context(tc.psum_pool(name="hop_banks", bufs=2))
         flip_banks = ctx.enter_context(tc.psum_pool(name="flip_banks", bufs=2))
 
-        x_sb = held.tile([P, S], BF16, name="x_sb")
-        nc.scalar.dma_start(x_sb[:], x)
+        x_sb = []
+        for s in range(S_PIECES):
+            x_piece = held.tile([P, COLS], BF16, name=f"x{s}")
+            nc.scalar.dma_start(x_piece[:], x[:, piece(s)])
+            x_sb.append(x_piece)
         bias = held.tile([P, M_BLOCKS], F32, name="bias")
         with nc.allow_non_contiguous_dma(reason="one bias value to a partition"):
             nc.scalar.dma_start(bias[:], b.rearrange("(a p) o -> p (a o)", p=P))
         offsets = held.tile([P, N // 16], U16, name="offsets")
         nc.sync.dma_start(offsets[:], offs)
 
-        lt_blocks = lt.rearrange("(p k) s -> p k s", k=S_BLOCKS)
-        first_blocks = list(range(0, S_BLOCKS - LT_PAIR, LT_PAIR)) + list(range(S_BLOCKS - LT_PAIR, S_BLOCKS))
         lt_sb = []
-        for n, k in enumerate(first_blocks):
-            count = (first_blocks + [S_BLOCKS])[n + 1] - k
-            lt_tile = held.tile([P, count, S], BF16, name=f"lt{k}")
-            nc.sync.dma_start(lt_tile[:], lt_blocks[:, k : k + count, :])
-            lt_sb.extend([lt_tile[:, i, :] for i in range(count)])
+        for t in range(S_BLOCKS):
+            lt_tile = held.tile([P, S], BF16, name=f"lt{t}")
+            nc.sync.dma_start(lt_tile[:], lt[block(t), :])
+            lt_sb.append(lt_tile)
 
         w_h0 = held.tile([P, M], BF16, name="w_h0")
         nc.sync.dma_start(w_h0[:], w[0:P, :])
@@ -85,41 +86,41 @@ def tile_net_b_kernel(tc, x, lt, kt, w, b, offs, out):
             else:
                 nc.scalar.copy(target, bank)
 
-        def flip_blocks(blocks):
+        def flip_blocks(source):
             bank = flip_banks.tile([P, QUAD, P], BF16, name="flip_bank")
             for q in range(QUAD):
-                nc.tensor.transpose(bank[:, q, :], blocks[q], identity[:])
+                nc.tensor.transpose(bank[:, q, :], source[:, block(q)], identity[:])
             return bank
 
         def flipped(n, source, name):
             result = held.tile([P, QUAD, P], BF16, name=name)
-            copy_out(n, result[:], flip_blocks([source[:, block(q)] for q in range(QUAD)])[:])
+            copy_out(n, result[:], flip_blocks(source)[:])
             return result
 
-        x_blocks = x_sb[:].rearrange("d (p k) -> d k p", k=S_BLOCKS)
-        xd_banks = []
-        xT = []
-        for g in range(S_PIECES):
-            xd_bank = long_banks.tile([P, COLS], F32, name=f"xd_bank{g}", tag="long")
-            nc.tensor.matmul(xd_bank[:], identity[:], x_sb[:, piece(g)], start=True, stop=False)
-            xd_banks.append(xd_bank)
-            scaled = held.tile([P, QUAD, P], BF16, name=f"xT{g}")
-            nc.vector.tensor_scalar_mul(
-                scaled[:], flip_blocks([x_blocks[:, QUAD * g + q, :] for q in range(QUAD)])[:], -TAU
+        xd_banks = [long_banks.tile([P, COLS], F32, name=f"xd_bank{s}", tag="long") for s in range(S_PIECES)]
+        xT = [flipped(0, x_sb[0], "xT0")]
+
+        def add_block(t, s):
+            nc.tensor.matmul(
+                xd_banks[s][:],
+                xT[t // QUAD][:, t % QUAD, :],
+                lt_sb[t][:, piece(s)],
+                start=(t == 0),
+                stop=(t == S_BLOCKS - 1),
             )
-            xT.append(scaled)
-        for k in range(S_BLOCKS):
+
+        for t in range(S_BLOCKS - LAST):
+            if t % QUAD == 0 and len(xT) < S_PIECES:
+                xT.append(flipped(0, x_sb[len(xT)], f"xT{len(xT)}"))
             for s in range(S_PIECES):
-                nc.tensor.matmul(
-                    xd_banks[s][:],
-                    xT[k // QUAD][:, k % QUAD, :],
-                    lt_sb[k][:, piece(s)],
-                    start=False,
-                    stop=(k == S_BLOCKS - 1),
-                )
+                add_block(t, s)
         xd = held.tile([P, S], BF16, name="xd")
         for s in range(S_PIECES):
-            copy_out(s, xd[:, piece(s)], xd_banks[s][:])
+            for t in range(S_BLOCKS - LAST, S_BLOCKS):
+                add_block(t, s)
+            nc.vector.scalar_tensor_tensor(
+                out=xd[:, piece(s)], in0=xd_banks[s][:], scalar=-TAU, in1=x_sb[s][:], op0=MULT, op1=ADD
+            )
 
         def picked(j):
             return xd[:].indirect(offsets[:, j * (COLS // 16) : (j + 1) * (COLS // 16)])

@@ -56,10 +56,17 @@ def tile_net_b_kernel(tc, x, lt, kt, w, b, offs, out):
         nc.sync.dma_start(offsets[:], offs)
 
         lt_sb = []
-        for t in range(S_BLOCKS):
+        for t in range(S_BLOCKS - LAST):
             lt_tile = held.tile([P, S], BF16, name=f"lt{t}")
             nc.sync.dma_start(lt_tile[:], lt[block(t), :])
             lt_sb.append(lt_tile)
+        lt_last = []
+        for s in range(S_PIECES):
+            lt_tile = held.tile([P, LAST, COLS], BF16, name=f"lt_last{s}")
+            nc.sync.dma_start(
+                lt_tile[:], lt[(S_BLOCKS - LAST) * P : S, piece(s)].rearrange("(i p) c -> p i c", p=P)
+            )
+            lt_last.append(lt_tile)
 
         w_h0 = held.tile([P, M], BF16, name="w_h0")
         nc.sync.dma_start(w_h0[:], w[0:P, :])
@@ -101,10 +108,14 @@ def tile_net_b_kernel(tc, x, lt, kt, w, b, offs, out):
         xT = [flipped(0, x_sb[0], "xT0")]
 
         def add_block(t, s):
+            if t < S_BLOCKS - LAST:
+                lt_part = lt_sb[t][:, piece(s)]
+            else:
+                lt_part = lt_last[s][:, t - (S_BLOCKS - LAST), :]
             nc.tensor.matmul(
                 xd_banks[s][:],
                 xT[t // QUAD][:, t % QUAD, :],
-                lt_sb[t][:, piece(s)],
+                lt_part,
                 start=(t == 0),
                 stop=(t == S_BLOCKS - 1),
             )

@@ -19,12 +19,13 @@ N_PIECES = N // COLS
 M_BLOCKS = M // P
 CAT_BLOCKS = 1 + NK + NK * NK
 LAST = 2
+XD_PARTS = [(2 * COLS, COLS), (0, COLS), (3 * COLS, COLS), (COLS, COLS // 2), (COLS + COLS // 2, COLS // 2)]
 
 FLOPS = 2 * (P * S * S + NK * P * N * N + NK * NK * P * N * N + CAT_BLOCKS * P * M * N)
 
 BF16, F32, U16 = mybir.dt.bfloat16, mybir.dt.float32, mybir.dt.uint16
 MULT, ADD = mybir.AluOpType.mult, mybir.AluOpType.add
-TANH = mybir.ActivationFunctionType.Tanh
+TANH, COPY = mybir.ActivationFunctionType.Tanh, mybir.ActivationFunctionType.Copy
 
 
 def piece(n):
@@ -61,10 +62,10 @@ def tile_net_b_kernel(tc, x, lt, kt, w, b, offs, out):
             nc.sync.dma_start(lt_tile[:], lt[block(t), :])
             lt_sb.append(lt_tile)
         lt_last = []
-        for s in range(S_PIECES):
-            lt_tile = held.tile([P, LAST, COLS], BF16, name=f"lt_last{s}")
+        for n, (first, count) in enumerate(XD_PARTS):
+            lt_tile = held.tile([P, LAST, count], BF16, name=f"lt_last{n}")
             nc.sync.dma_start(
-                lt_tile[:], lt[(S_BLOCKS - LAST) * P : S, piece(s)].rearrange("(i p) c -> p i c", p=P)
+                lt_tile[:], lt[(S_BLOCKS - LAST) * P : S, first : first + count].rearrange("(i p) c -> p i c", p=P)
             )
             lt_last.append(lt_tile)
 
@@ -86,6 +87,8 @@ def tile_net_b_kernel(tc, x, lt, kt, w, b, offs, out):
 
         identity = held.tile([P, P], BF16, name="identity")
         make_identity(nc, identity[:])
+        minus_two = held.tile([P, P], BF16, name="minus_two")
+        nc.vector.tensor_scalar_mul(minus_two[:], identity[:], -1.0 / TAU)
 
         def copy_out(n, target, bank):
             if n % 2 == 0:
@@ -105,51 +108,81 @@ def tile_net_b_kernel(tc, x, lt, kt, w, b, offs, out):
             return result
 
         xd_banks = [long_banks.tile([P, COLS], F32, name=f"xd_bank{s}", tag="long") for s in range(S_PIECES)]
-        xT = [flipped(0, x_sb[0], "xT0")]
+        xd_banks.append(hop_banks.tile([P, COLS], F32, name="hop_bank"))
+        begun = set()
 
-        def add_block(t, s):
+        def add_to_part(n, weights, moving, last):
+            nc.tensor.matmul(xd_banks[n][:, 0 : XD_PARTS[n][1]], weights, moving, start=(n not in begun), stop=last)
+            begun.add(n)
+
+        def x_part(n):
+            first, count = XD_PARTS[n]
+            return x_sb[first // COLS][:, first % COLS : first % COLS + count]
+
+        def add_block(t, n):
+            first, count = XD_PARTS[n]
             if t < S_BLOCKS - LAST:
-                lt_part = lt_sb[t][:, piece(s)]
+                lt_part = lt_sb[t][:, first : first + count]
             else:
-                lt_part = lt_last[s][:, t - (S_BLOCKS - LAST), :]
-            nc.tensor.matmul(
-                xd_banks[s][:],
-                xT[t // QUAD][:, t % QUAD, :],
-                lt_part,
-                start=(t == 0),
-                stop=(t == S_BLOCKS - 1),
-            )
+                lt_part = lt_last[n][:, t - (S_BLOCKS - LAST), :]
+            add_to_part(n, xT[t // QUAD][:, t % QUAD, :], lt_part, t == S_BLOCKS - 1)
 
+        xT = []
+
+        def take_x_piece():
+            g = len(xT)
+            xT.append(flipped(0, x_sb[g], f"xT{g}"))
+            for n in range(1, len(XD_PARTS), 2):
+                if XD_PARTS[n][0] // COLS == g:
+                    add_to_part(n, minus_two[:], x_part(n), False)
+
+        take_x_piece()
         for t in range(S_BLOCKS - LAST):
+            for n in range(len(XD_PARTS)):
+                add_block(t, n)
             if t % QUAD == 0 and len(xT) < S_PIECES:
-                xT.append(flipped(0, x_sb[len(xT)], f"xT{len(xT)}"))
-            for s in range(S_PIECES):
-                add_block(t, s)
+                take_x_piece()
         xd = held.tile([P, S], BF16, name="xd")
-        for s in range(S_PIECES):
+        for n, (first, count) in enumerate(XD_PARTS):
             for t in range(S_BLOCKS - LAST, S_BLOCKS):
-                add_block(t, s)
-            nc.vector.scalar_tensor_tensor(
-                out=xd[:, piece(s)], in0=xd_banks[s][:], scalar=-TAU, in1=x_sb[s][:], op0=MULT, op1=ADD
-            )
+                add_block(t, n)
+            if n % 2 == 0:
+                nc.vector.scalar_tensor_tensor(
+                    out=xd[:, first : first + count],
+                    in0=xd_banks[n][:, 0:count],
+                    scalar=-TAU,
+                    in1=x_part(n),
+                    op0=MULT,
+                    op1=ADD,
+                )
+            else:
+                nc.scalar.activation(xd[:, first : first + count], xd_banks[n][:, 0:count], COPY, scale=-TAU)
 
-        def picked(j):
-            return xd[:].indirect(offsets[:, j * (COLS // 16) : (j + 1) * (COLS // 16)])
+        def picked(first, count):
+            return xd[:].indirect(offsets[:, first // 16 : (first + count) // 16])
 
-        def open_encoder(j, m):
+        def open_encoder(bank, m, first, count):
+            nc.tensor.matmul(bank[:, 0:count], w_h0[:, block(m)], picked(first, count), start=True, stop=False)
+            return (bank, m, first, count)
+
+        def open_piece(j, m):
             bank = long_banks.tile([P, COLS], F32, name=f"out_bank{m}", tag="long")
-            nc.tensor.matmul(bank[:], w_h0[:, block(m)], picked(j), start=True, stop=False)
-            return bank
+            return open_encoder(bank, m, j * COLS, COLS)
 
-        def close_encoder(j, banks, layers):
-            for m in range(M_BLOCKS):
+        def close_encoder(j, opened, layers):
+            for bank, m, first, count in opened:
+                inside = slice(first - j * COLS, first - j * COLS + count)
                 for f, layer in enumerate(layers):
                     nc.tensor.matmul(
-                        banks[m][:], w_rest[:, f, block(m)], layer[j][:], start=False, stop=(f == len(layers) - 1)
+                        bank[:, 0:count],
+                        w_rest[:, f, block(m)],
+                        layer[j][:, inside],
+                        start=False,
+                        stop=(f == len(layers) - 1),
                     )
                 out_sb = staged.tile([P, COLS], F32, name="out_sb")
-                nc.scalar.activation(out_sb[:], banks[m][:], TANH, bias=bias[:, m : m + 1])
-                nc.sync.dma_start(out[block(m), piece(j)], out_sb[:])
+                nc.scalar.activation(out_sb[:, 0:count], bank[:, 0:count], TANH, bias=bias[:, m : m + 1])
+                nc.sync.dma_start(out[block(m), first : first + count], out_sb[:, 0:count])
 
         def hop(flipped_pieces, a, j, name):
             bank = hop_banks.tile([P, COLS], F32, name="hop_bank")
@@ -168,15 +201,15 @@ def tile_net_b_kernel(tc, x, lt, kt, w, b, offs, out):
         h0_banks = []
         for j in range(N_PIECES):
             bank = hop_banks.tile([P, COLS], F32, name="hop_bank")
-            nc.tensor.matmul(bank[:], identity[:], picked(j), start=True, stop=True)
+            nc.tensor.matmul(bank[:], identity[:], picked(j * COLS, COLS), start=True, stop=True)
             h0_banks.append(bank)
-        out_banks = [open_encoder(0, m) for m in range(M_BLOCKS // 2)]
+        opened = [open_piece(0, m) for m in range(M_BLOCKS // 2)]
         h0T = []
         for j in range(N_PIECES):
             h0 = held.tile([P, COLS], BF16, name=f"h0_{j}")
             copy_out(j, h0[:], h0_banks[j][:])
             h0T.append(flipped(j, h0, f"h0T{j}"))
-        out_banks.extend([open_encoder(0, m) for m in range(M_BLOCKS // 2, M_BLOCKS)])
+        opened.extend([open_piece(0, m) for m in range(M_BLOCKS // 2, M_BLOCKS)])
 
         h1 = [[None] * N_PIECES for a in range(NK)]
         h1T = [[None] * N_PIECES for a in range(NK)]
@@ -202,5 +235,8 @@ def tile_net_b_kernel(tc, x, lt, kt, w, b, offs, out):
                     if late:
                         flip_oldest()
             if j > 0:
-                out_banks = [open_encoder(j, m) for m in range(M_BLOCKS)]
-            close_encoder(j, out_banks, h1 + h2)
+                opened = [open_piece(j, m) for m in range(M_BLOCKS - 1)]
+                for half in range(2):
+                    bank = hop_banks.tile([P, COLS], F32, name="hop_bank")
+                    opened.append(open_encoder(bank, M_BLOCKS - 1, j * COLS + half * (COLS // 2), COLS // 2))
+            close_encoder(j, opened, h1 + h2)

@@ -50,9 +50,6 @@ def tile_net_b_kernel(tc, x, lt, kt, w, b, offs, out):
             x_piece = held.tile([P, COLS], BF16, name=f"x{s}")
             nc.scalar.dma_start(x_piece[:], x[:, piece(s)])
             x_sb.append(x_piece)
-        bias = held.tile([P, M_BLOCKS], F32, name="bias")
-        with nc.allow_non_contiguous_dma(reason="one bias value to a partition"):
-            nc.scalar.dma_start(bias[:], b.rearrange("(a p) o -> p (a o)", p=P))
         offsets = held.tile([P, N // 16], U16, name="offsets")
         nc.sync.dma_start(offsets[:], offs)
 
@@ -84,6 +81,9 @@ def tile_net_b_kernel(tc, x, lt, kt, w, b, offs, out):
 
         w_rest = held.tile([P, CAT_BLOCKS - 1, M], BF16, name="w_rest")
         nc.sync.dma_start(w_rest[:], w[P : CAT_BLOCKS * P, :].rearrange("(f p) m -> p f m", p=P))
+        bias = held.tile([P, M_BLOCKS], F32, name="bias")
+        with nc.allow_non_contiguous_dma(reason="one bias value to a partition"):
+            nc.sync.dma_start(bias[:], b.rearrange("(a p) o -> p (a o)", p=P))
 
         identity = held.tile([P, P], BF16, name="identity")
         make_identity(nc, identity[:])

@@ -125,13 +125,19 @@ def tile_net_b_kernel(tc, x, lt, kt, w, b, offs, out):
                 lt_part = lt_sb[t][:, first : first + count]
             else:
                 lt_part = lt_last[n][:, t - (S_BLOCKS - LAST), :]
-            add_to_part(n, xT[t // QUAD][:, t % QUAD, :], lt_part, t == S_BLOCKS - 1)
+            add_to_part(n, xT[t // 2][:, t % 2, :], lt_part, t == S_BLOCKS - 1)
 
         xT = []
 
         def take_x_piece():
-            g = len(xT)
-            xT.append(flipped(0, x_sb[g], f"xT{g}"))
+            g = len(xT) // 2
+            for half in range(2):
+                bank = flip_banks.tile([P, 2, P], BF16, name="flip_bank")
+                for q in range(2):
+                    nc.tensor.transpose(bank[:, q, :], x_sb[g][:, block(2 * half + q)], identity[:])
+                pair = held.tile([P, 2, P], BF16, name=f"xT{len(xT)}")
+                copy_out(half, pair[:], bank[:])
+                xT.append(pair)
             for n in range(1, len(XD_PARTS), 2):
                 if XD_PARTS[n][0] // COLS == g:
                     add_to_part(n, minus_two[:], x_part(n), False)
@@ -140,7 +146,7 @@ def tile_net_b_kernel(tc, x, lt, kt, w, b, offs, out):
         for t in range(S_BLOCKS - LAST):
             for n in range(len(XD_PARTS)):
                 add_block(t, n)
-            if t % QUAD == 0 and len(xT) < S_PIECES:
+            if t % QUAD == 0 and len(xT) < S_BLOCKS // 2:
                 take_x_piece()
         xd = held.tile([P, S], BF16, name="xd")
         for n, (first, count) in enumerate(XD_PARTS):

@@ -45,11 +45,11 @@ def tile_net_b_kernel(tc, x, lt, kt, w, b, offs, out):
         hop_banks = ctx.enter_context(tc.psum_pool(name="hop_banks", bufs=2))
         flip_banks = ctx.enter_context(tc.psum_pool(name="flip_banks", bufs=2))
 
-        x_sb = []
-        for s in range(S_PIECES):
-            x_piece = held.tile([P, COLS], BF16, name=f"x{s}")
-            nc.scalar.dma_start(x_piece[:], x[:, piece(s)])
-            x_sb.append(x_piece)
+        x_first = held.tile([P, COLS], BF16, name="x_first")
+        nc.scalar.dma_start(x_first[:], x[:, piece(0)])
+        x_rest = held.tile([P, S - COLS], BF16, name="x_rest")
+        nc.scalar.dma_start(x_rest[:], x[:, COLS:S])
+        x_sb = [x_first[:]] + [x_rest[:, piece(s - 1)] for s in range(1, S_PIECES)]
         offsets = held.tile([P, N // 16], U16, name="offsets")
         nc.sync.dma_start(offsets[:], offs)
 

from contextlib import ExitStack

import concourse.mybir as mybir
from concourse.masks import make_identity

P = 128
S = 2048
N = 1024
NK = 2
M = 512
TAU = 0.5
COLS = 512
QUAD = COLS // P

S_BLOCKS = S // P
S_PIECES = S // COLS
N_BLOCKS = N // P
N_PIECES = N // COLS
M_BLOCKS = M // P
CAT_BLOCKS = 1 + NK + NK * NK
LAST = 2
XD_PARTS = [(2 * COLS, COLS), (0, COLS), (3 * COLS, COLS), (COLS, COLS // 2), (COLS + COLS // 2, COLS // 2)]

FLOPS = 2 * (P * S * S + NK * P * N * N + NK * NK * P * N * N + CAT_BLOCKS * P * M * N)

BF16, F32, U16 = mybir.dt.bfloat16, mybir.dt.float32, mybir.dt.uint16
MULT, ADD = mybir.AluOpType.mult, mybir.AluOpType.add
TANH, COPY = mybir.ActivationFunctionType.Tanh, mybir.ActivationFunctionType.Copy


def piece(n):
    return slice(n * COLS, (n + 1) * COLS)


def block(n):
    return slice(n * P, (n + 1) * P)


def tile_net_b_kernel(tc, x, lt, kt, w, b, offs, out):
    nc = tc.nc
    with ExitStack() as ctx:
        held = ctx.enter_context(tc.tile_pool(name="held", bufs=1))
        staged = ctx.enter_context(tc.tile_pool(name="staged", bufs=4))
        long_banks = ctx.enter_context(tc.psum_pool(name="long_banks", bufs=4))
        hop_banks = ctx.enter_context(tc.psum_pool(name="hop_banks", bufs=2))
        flip_banks = ctx.enter_context(tc.psum_pool(name="flip_banks", bufs=2))

        x_first = held.tile([P, COLS], BF16, name="x_first")
        nc.scalar.dma_start(x_first[:], x[:, piece(0)])
        x_rest = held.tile([P, S - COLS], BF16, name="x_rest")
        nc.scalar.dma_start(x_rest[:], x[:, COLS:S])
        x_sb = [x_first[:]] + [x_rest[:, piece(s - 1)] for s in range(1, S_PIECES)]
        offsets = held.tile([P, N // 16], U16, name="offsets")
        nc.sync.dma_start(offsets[:], offs)

        lt_sb = []
        for t in range(S_BLOCKS - LAST):
            lt_tile = held.tile([P, S], BF16, name=f"lt{t}")
            nc.sync.dma_start(lt_tile[:], lt[block(t), :])
            lt_sb.append(lt_tile)
        lt_last = []
        for n, (first, count) in enumerate(XD_PARTS):
            lt_tile = held.tile([P, LAST, count], BF16, name=f"lt_last{n}")
            nc.sync.dma_start(
                lt_tile[:], lt[(S_BLOCKS - LAST) * P : S, first : first + count].rearrange("(i p) c -> p i c", p=P)
            )
            lt_last.append(lt_tile)

        w_h0 = held.tile([P, M], BF16, name="w_h0")
        nc.sync.dma_start(w_h0[:], w[0:P, :])

        kt_sb = []
        for a in range(NK):
            kt_loads = kt[a].rearrange("(h k p) j -> h p k j", k=QUAD, p=P)
            halves = []
            for h in range(N_BLOCKS // QUAD):
                kt_tile = held.tile([P, QUAD, N], BF16, name=f"kt{a}{h}")
                nc.sync.dma_start(kt_tile[:], kt_loads[h])
                halves.append(kt_tile)
            kt_sb.append(halves)

        w_rest = held.tile([P, CAT_BLOCKS - 1, M], BF16, name="w_rest")
        nc.sync.dma_start(w_rest[:], w[P : CAT_BLOCKS * P, :].rearrange("(f p) m -> p f m", p=P))
        bias = held.tile([P, M_BLOCKS], F32, name="bias")
        with nc.allow_non_contiguous_dma(reason="one bias value to a partition"):
            nc.sync.dma_start(bias[:], b.rearrange("(a p) o -> p (a o)", p=P))

        identity = held.tile([P, P], BF16, name="identity")
        make_identity(nc, identity[:])
        minus_two = held.tile([P, P], BF16, name="minus_two")
        nc.vector.tensor_scalar_mul(minus_two[:], identity[:], -1.0 / TAU)

        def copy_out(n, target, bank):
            if n % 2 == 0:
                nc.vector.tensor_copy(target, bank)
            else:
                nc.scalar.copy(target, bank)

        def flip_blocks(source):
            bank = flip_banks.tile([P, QUAD, P], BF16, name="flip_bank")
            for q in range(QUAD):
                nc.tensor.transpose(bank[:, q, :], source[:, block(q)], identity[:])
            return bank

        def flipped(n, source, name):
            result = held.tile([P, QUAD, P], BF16, name=name)
            copy_out(n, result[:], flip_blocks(source)[:])
            return result

        xd_banks = [long_banks.tile([P, COLS], F32, name=f"xd_bank{s}", tag="long") for s in range(S_PIECES)]
        xd_banks.append(hop_banks.tile([P, COLS], F32, name="hop_bank"))
        begun = set()

        def add_to_part(n, weights, moving, last):
            nc.tensor.matmul(xd_banks[n][:, 0 : XD_PARTS[n][1]], weights, moving, start=(n not in begun), stop=last)
            begun.add(n)

        def x_part(n):
            first, count = XD_PARTS[n]
            return x_sb[first // COLS][:, first % COLS : first % COLS + count]

        def add_block(t, n):
            first, count = XD_PARTS[n]
            if t < S_BLOCKS - LAST:
                lt_part = lt_sb[t][:, first : first + count]
            else:
                lt_part = lt_last[n][:, t - (S_BLOCKS - LAST), :]
            add_to_part(n, xT[t // 2][:, t % 2, :], lt_part, t == S_BLOCKS - 1)

        xT = []

        def take_x_piece():
            g = len(xT) // 2
            for half in range(2):
                bank = flip_banks.tile([P, 2, P], BF16, name="flip_bank")
                for q in range(2):
                    nc.tensor.transpose(bank[:, q, :], x_sb[g][:, block(2 * half + q)], identity[:])
                pair = held.tile([P, 2, P], BF16, name=f"xT{len(xT)}")
                copy_out(half, pair[:], bank[:])
                xT.append(pair)
            for n in range(1, len(XD_PARTS), 2):
                if XD_PARTS[n][0] // COLS == g:
                    add_to_part(n, minus_two[:], x_part(n), False)

        take_x_piece()
        for t in range(S_BLOCKS - LAST):
            for n in range(len(XD_PARTS)):
                add_block(t, n)
            if t % QUAD == 0 and len(xT) < S_BLOCKS // 2:
                take_x_piece()
        xd = held.tile([P, S], BF16, name="xd")
        for n, (first, count) in enumerate(XD_PARTS):
            for t in range(S_BLOCKS - LAST, S_BLOCKS):
                add_block(t, n)
            if n % 2 == 0:
                nc.vector.scalar_tensor_tensor(
                    out=xd[:, first : first + count],
                    in0=xd_banks[n][:, 0:count],
                    scalar=-TAU,
                    in1=x_part(n),
                    op0=MULT,
                    op1=ADD,
                )
            else:
                nc.scalar.activation(xd[:, first : first + count], xd_banks[n][:, 0:count], COPY, scale=-TAU)

        def picked(first, count):
            return xd[:].indirect(offsets[:, first // 16 : (first + count) // 16])

        def open_encoder(bank, m, first, count):
            nc.tensor.matmul(bank[:, 0:count], w_h0[:, block(m)], picked(first, count), start=True, stop=False)
            return (bank, m, first, count)

        def open_piece(j, m):
            bank = long_banks.tile([P, COLS], F32, name=f"out_bank{m}", tag="long")
            return open_encoder(bank, m, j * COLS, COLS)

        def close_encoder(j, opened, layers):
            for bank, m, first, count in opened:
                inside = slice(first - j * COLS, first - j * COLS + count)
                for f, layer in enumerate(layers):
                    nc.tensor.matmul(
                        bank[:, 0:count],
                        w_rest[:, f, block(m)],
                        layer[j][:, inside],
                        start=False,
                        stop=(f == len(layers) - 1),
                    )
                out_sb = staged.tile([P, COLS], F32, name="out_sb")
                nc.scalar.activation(out_sb[:, 0:count], bank[:, 0:count], TANH, bias=bias[:, m : m + 1])
                nc.sync.dma_start(out[block(m), first : first + count], out_sb[:, 0:count])

        def hop(flipped_pieces, a, j, name):
            bank = hop_banks.tile([P, COLS], F32, name="hop_bank")
            for i in range(N_BLOCKS):
                nc.tensor.matmul(
                    bank[:],
                    flipped_pieces[i // QUAD][:, i % QUAD, :],
                    kt_sb[a][i // QUAD][:, i % QUAD, piece(j)],
                    start=(i == 0),
                    stop=(i == N_BLOCKS - 1),
                )
            result = held.tile([P, COLS], BF16, name=name)
            copy_out(j, result[:], bank[:])
            return result

        h0_banks = []
        for j in range(N_PIECES):
            bank = hop_banks.tile([P, COLS], F32, name="hop_bank")
            nc.tensor.matmul(bank[:], identity[:], picked(j * COLS, COLS), start=True, stop=True)
            h0_banks.append(bank)
        opened = [open_piece(0, m) for m in range(M_BLOCKS // 2)]
        h0T = []
        for j in range(N_PIECES):
            h0 = held.tile([P, COLS], BF16, name=f"h0_{j}")
            copy_out(j, h0[:], h0_banks[j][:])
            h0T.append(flipped(j, h0, f"h0T{j}"))
        opened.extend([open_piece(0, m) for m in range(M_BLOCKS // 2, M_BLOCKS)])

        h1 = [[None] * N_PIECES for a in range(NK)]
        h1T = [[None] * N_PIECES for a in range(NK)]
        late = []

        def flip_oldest():
            a, j = late[0]
            late.remove(late[0])
            h1T[a][j] = flipped(j, h1[a][j], f"h1T{a}{j}")

        for a in range(NK):
            for j in range(N_PIECES):
                h1[a][j] = hop(h0T, a, j, f"h1_{a}{j}")
                late.append((a, j))
                if len(late) == 2:
                    flip_oldest()

        h2 = [[None] * N_PIECES for r in range(NK * NK)]
        for j in range(N_PIECES):
            for e in range(NK):
                for a in range(NK):
                    h2[NK * a + e][j] = hop(h1T[e], a, j, f"h2_{a}{e}{j}")
                    if late:
                        flip_oldest()
            if j > 0:
                opened = [open_piece(j, m) for m in range(M_BLOCKS - 1)]
                for half in range(2):
                    bank = hop_banks.tile([P, COLS], F32, name="hop_bank")
                    opened.append(open_encoder(bank, M_BLOCKS - 1, j * COLS + half * (COLS // 2), COLS // 2))
            close_encoder(j, opened, h1 + h2)
